import numpy as np
import ml_dtypes

BF16 = ml_dtypes.bfloat16


def bf(x):
    return np.asarray(x, np.float32).astype(BF16)


def f32(x):
    return np.asarray(x, np.float32)


def f64(x):
    return np.asarray(x).astype(np.float64)


def striped(idx):
    return np.tile(idx.reshape(-1, 16).T, (8, 1))


C, S, N, H = 1024, 512, 384, 256


def setup_inputs():
    return {"x": f32(np.random.standard_normal((C, S))), "hid": bf(np.abs(np.random.standard_normal((H, C)))), "w_s": bf(0.5 * np.random.standard_normal((H, N)) / np.sqrt(H)), "w_t": bf(np.random.standard_normal((H, N)) / np.sqrt(H)), "offs": striped(np.random.permutation(S)[:N])}


def reference(x, hid, w_s, w_t, offs):
    idx = offs[:16].T.reshape(-1)
    sc = f64(hid).T @ f64(w_s)
    tr = f64(hid).T @ f64(w_t)
    return f64(x)[:, idx] * np.exp(sc) + tr

@@ -1,0 +1,115 @@
+import concourse.mybir as mybir
+from concourse.masks import make_identity
+
+P = 128
+C, S, N, H = 1024, 512, 384, 256
+BLOCKS = C // P
+KSTEPS = H // P
+HID_PIECE = 2
+TR_AHEAD = 3
+SC_AHEAD = TR_AHEAD + 1
+TENSOR_ADDS = range(BLOCKS - 4, BLOCKS - 1)
+
+BF16, F32, U16 = mybir.dt.bfloat16, mybir.dt.float32, mybir.dt.uint16
+MULT, ADD = mybir.AluOpType.mult, mybir.AluOpType.add
+EXP = mybir.ActivationFunctionType.Exp
+
+FLOPS = 2 * 2 * C * H * N
+BYTES = 4 * C * N + 2 * H * C + 2 * 2 * H * N + 2 * P * (N // 16) + 4 * C * N
+
+
+def tile_affine_coupling_layer_kernel(tc, x, hid, w_s, w_t, offs, out):
+    nc = tc.nc
+    with (
+        tc.tile_pool(name="held", bufs=1) as held,
+        tc.tile_pool(name="work", bufs=SC_AHEAD + 1) as work,
+        tc.psum_pool(name="psum_sc", bufs=3) as psum_sc,
+        tc.psum_pool(name="psum_tr", bufs=5) as psum_tr,
+    ):
+        offsets = held.tile([P, N // 16], U16, name="offsets")
+
+        hid_pieces = hid.rearrange("(k p) (g c) -> g p k c", p=P, c=HID_PIECE * P)
+        x_blocks = x.rearrange("(b p) s -> b p s", p=P)
+        out_blocks = out.rearrange("(b p) n -> b p n", p=P)
+
+        ws_sb = held.tile([P, KSTEPS, N], BF16, name="ws_sb")
+        wt_sb = held.tile([P, KSTEPS, N], BF16, name="wt_sb")
+        hid_sb = [
+            held.tile([P, KSTEPS, HID_PIECE * P], BF16, name=f"hid{g}")
+            for g in range(BLOCKS // HID_PIECE)
+        ]
+        x_sb = [held.tile([P, S], F32, name=f"x{b}") for b in range(BLOCKS)]
+
+        nc.sync.dma_start(hid_sb[0][:], hid_pieces[0])
+        nc.sync.dma_start(ws_sb[:], w_s.rearrange("(k p) n -> p k n", p=P))
+        for b in range(BLOCKS):
+            nc.sync.dma_start(x_sb[b][:], x_blocks[b])
+            if b == 0:
+                nc.sync.dma_start(offsets[:], offs)
+                nc.sync.dma_start(wt_sb[:], w_t.rearrange("(k p) n -> p k n", p=P))
+            ahead = b + 2
+            if ahead % HID_PIECE == 0 and ahead < BLOCKS:
+                nc.sync.dma_start(hid_sb[ahead // HID_PIECE][:], hid_pieces[ahead // HID_PIECE])
+
+        ident = held.tile([P, P], F32, name="ident")
+        make_identity(nc, ident[:])
+
+        scales = {}
+        translations = {}
+
+        def hid_of(b, k):
+            first = (b % HID_PIECE) * P
+            return hid_sb[b // HID_PIECE][:, k, first : first + P]
+
+        def logits(b):
+            sc = psum_sc.tile([P, N], F32, name="sc")
+            for k in range(KSTEPS):
+                nc.tensor.matmul(
+                    sc[:], hid_of(b, k), ws_sb[:, k, :], start=(k == 0), stop=(k == KSTEPS - 1)
+                )
+            scale = work.tile([P, N], F32, name="scale")
+            nc.scalar.activation(scale[:], sc[:], EXP)
+            scales[b] = scale
+
+        def translation(b):
+            tr = psum_tr.tile([P, N], F32, name="tr")
+            for k in range(KSTEPS):
+                nc.tensor.matmul(
+                    tr[:],
+                    hid_of(b, k),
+                    wt_sb[:, k, :],
+                    start=(k == 0),
+                    stop=(k == KSTEPS - 1 and b not in TENSOR_ADDS),
+                )
+            if b in TENSOR_ADDS:
+                translations[b] = tr
+            else:
+                tr_sb = work.tile([P, N], F32, name="tr_sb")
+                nc.scalar.copy(tr_sb[:], tr[:])
+                translations[b] = tr_sb
+
+        def read_outs(b):
+            if b + 1 < BLOCKS:
+                logits(b + 1)
+            translation(b)
+
+        logits(0)
+        for b in range(TR_AHEAD):
+            read_outs(b)
+
+        for b in range(BLOCKS):
+            if b + TR_AHEAD < BLOCKS:
+                read_outs(b + TR_AHEAD)
+            tr = translations[b]
+
+            prod = work.tile([P, N], F32, name="prod")
+            nc.vector.tensor_tensor(prod[:], x_sb[b][:].indirect(offsets[:]), scales[b][:], MULT)
+
+            res = work.tile([P, N], F32, name="res")
+            if b in TENSOR_ADDS:
+                nc.tensor.matmul(tr[:], ident[:], prod[:], start=False, stop=True)
+                nc.scalar.copy(res[:], tr[:])
+                nc.scalar.dma_start(out_blocks[b], res[:])
+            else:
+                nc.vector.tensor_tensor(res[:], prod[:], tr[:], ADD)
+                nc.sync.dma_start(out_blocks[b], res[:])

@@ -28,7 +28,7 @@ def tile_affine_coupling_layer_kernel(tc, x, hid, w_s, w_t, offs, out):
     ):
         offsets = held.tile([P, N // 16], U16, name="offsets")
 
-        hid_pieces = hid.rearrange("(k p) (g c) -> g p k c", p=P, c=HID_PIECE * P)
+        hid_pieces = hid.rearrange("(p k) (g c) -> g p k c", p=P, c=HID_PIECE * P)
         x_blocks = x.rearrange("(b p) s -> b p s", p=P)
         out_blocks = out.rearrange("(b p) n -> b p n", p=P)
 
@@ -41,12 +41,12 @@ def tile_affine_coupling_layer_kernel(tc, x, hid, w_s, w_t, offs, out):
         x_sb = [held.tile([P, S], F32, name=f"x{b}") for b in range(BLOCKS)]
 
         nc.sync.dma_start(hid_sb[0][:], hid_pieces[0])
-        nc.sync.dma_start(ws_sb[:], w_s.rearrange("(k p) n -> p k n", p=P))
+        nc.sync.dma_start(ws_sb[:], w_s.rearrange("(p k) n -> p k n", p=P))
         for b in range(BLOCKS):
             nc.sync.dma_start(x_sb[b][:], x_blocks[b])
             if b == 0:
                 nc.sync.dma_start(offsets[:], offs)
-                nc.sync.dma_start(wt_sb[:], w_t.rearrange("(k p) n -> p k n", p=P))
+                nc.sync.dma_start(wt_sb[:], w_t.rearrange("(p k) n -> p k n", p=P))
             ahead = b + 2
             if ahead % HID_PIECE == 0 and ahead < BLOCKS:
                 nc.sync.dma_start(hid_sb[ahead // HID_PIECE][:], hid_pieces[ahead // HID_PIECE])

@@ -40,8 +40,11 @@ def tile_affine_coupling_layer_kernel(tc, x, hid, w_s, w_t, offs, out):
         ]
         x_sb = [held.tile([P, S], F32, name=f"x{b}") for b in range(BLOCKS)]
 
-        nc.sync.dma_start(hid_sb[0][:], hid_pieces[0])
-        nc.sync.dma_start(ws_sb[:], w_s.rearrange("(p k) n -> p k n", p=P))
+        ws_steps = w_s.rearrange("(p k) n -> k p n", p=P)
+        hid_first_steps = hid.rearrange("(p k) c -> k p c", p=P)[:, :, 0 : HID_PIECE * P]
+        for k in range(KSTEPS):
+            nc.sync.dma_start(hid_sb[0][:, k, :], hid_first_steps[k])
+            nc.sync.dma_start(ws_sb[:, k, :], ws_steps[k])
         for b in range(BLOCKS):
             nc.sync.dma_start(x_sb[b][:], x_blocks[b])
             if b == 0:

@@ -66,9 +66,10 @@ def tile_affine_coupling_layer_kernel(tc, x, hid, w_s, w_t, offs, out):
 
         def logits(b):
             sc = psum_sc.tile([P, N], F32, name="sc")
-            for k in range(KSTEPS):
+            steps = range(KSTEPS) if b == 0 else range(KSTEPS - 1, -1, -1)
+            for i, k in enumerate(steps):
                 nc.tensor.matmul(
-                    sc[:], hid_of(b, k), ws_sb[:, k, :], start=(k == 0), stop=(k == KSTEPS - 1)
+                    sc[:], hid_of(b, k), ws_sb[:, k, :], start=(i == 0), stop=(i == KSTEPS - 1)
                 )
             scale = work.tile([P, N], F32, name="scale")
             nc.scalar.activation(scale[:], sc[:], EXP)

@@ -50,9 +50,10 @@ def tile_affine_coupling_layer_kernel(tc, x, hid, w_s, w_t, offs, out):
             if b == 0:
                 nc.sync.dma_start(offsets[:], offs)
                 nc.sync.dma_start(wt_sb[:], w_t.rearrange("(p k) n -> p k n", p=P))
-            ahead = b + 2
-            if ahead % HID_PIECE == 0 and ahead < BLOCKS:
-                nc.sync.dma_start(hid_sb[ahead // HID_PIECE][:], hid_pieces[ahead // HID_PIECE])
+            elif b == 1:
+                nc.sync.dma_start(hid_sb[1][:], hid_pieces[1])
+            elif b % HID_PIECE == 0 and b + HID_PIECE < BLOCKS:
+                nc.sync.dma_start(hid_sb[b // HID_PIECE + 1][:], hid_pieces[b // HID_PIECE + 1])
 
         ident = held.tile([P, P], F32, name="ident")
         make_identity(nc, ident[:])

@@ -8,7 +8,7 @@ KSTEPS = H // P
 HID_PIECE = 2
 TR_AHEAD = 3
 SC_AHEAD = TR_AHEAD + 1
-TENSOR_ADDS = range(BLOCKS - 4, BLOCKS - 1)
+TENSOR_COLUMNS = [0] * (BLOCKS - 4) + [N, N, N // 2, 0]
 
 BF16, F32, U16 = mybir.dt.bfloat16, mybir.dt.float32, mybir.dt.uint16
 MULT, ADD = mybir.AluOpType.mult, mybir.AluOpType.add
@@ -59,6 +59,7 @@ def tile_affine_coupling_layer_kernel(tc, x, hid, w_s, w_t, offs, out):
         make_identity(nc, ident[:])
 
         scales = {}
+        open_sums = {}
         translations = {}
 
         def hid_of(b, k):
@@ -77,21 +78,25 @@ def tile_affine_coupling_layer_kernel(tc, x, hid, w_s, w_t, offs, out):
             scales[b] = scale
 
         def translation(b):
-            tr = psum_tr.tile([P, N], F32, name="tr")
-            for k in range(KSTEPS):
-                nc.tensor.matmul(
-                    tr[:],
-                    hid_of(b, k),
-                    wt_sb[:, k, :],
-                    start=(k == 0),
-                    stop=(k == KSTEPS - 1 and b not in TENSOR_ADDS),
-                )
-            if b in TENSOR_ADDS:
-                translations[b] = tr
-            else:
-                tr_sb = work.tile([P, N], F32, name="tr_sb")
-                nc.scalar.copy(tr_sb[:], tr[:])
-                translations[b] = tr_sb
+            cut = TENSOR_COLUMNS[b]
+            for first, end, tensor_adds in ((0, cut, True), (cut, N, False)):
+                if first == end:
+                    continue
+                tr = psum_tr.tile([P, end - first], F32, name="tr")
+                for k in range(KSTEPS):
+                    nc.tensor.matmul(
+                        tr[:],
+                        hid_of(b, k),
+                        wt_sb[:, k, first:end],
+                        start=(k == 0),
+                        stop=(k == KSTEPS - 1 and not tensor_adds),
+                    )
+                if tensor_adds:
+                    open_sums[b] = tr
+                else:
+                    tr_sb = work.tile([P, end - first], F32, name="tr_sb")
+                    nc.scalar.copy(tr_sb[:], tr[:])
+                    translations[b] = tr_sb
 
         def read_outs(b):
             if b + 1 < BLOCKS:
@@ -105,16 +110,16 @@ def tile_affine_coupling_layer_kernel(tc, x, hid, w_s, w_t, offs, out):
         for b in range(BLOCKS):
             if b + TR_AHEAD < BLOCKS:
                 read_outs(b + TR_AHEAD)
-            tr = translations[b]
+            cut = TENSOR_COLUMNS[b]
 
             prod = work.tile([P, N], F32, name="prod")
             nc.vector.tensor_tensor(prod[:], x_sb[b][:].indirect(offsets[:]), scales[b][:], MULT)
 
             res = work.tile([P, N], F32, name="res")
-            if b in TENSOR_ADDS:
-                nc.tensor.matmul(tr[:], ident[:], prod[:], start=False, stop=True)
-                nc.scalar.copy(res[:], tr[:])
-                nc.scalar.dma_start(out_blocks[b], res[:])
-            else:
-                nc.vector.tensor_tensor(res[:], prod[:], tr[:], ADD)
-                nc.sync.dma_start(out_blocks[b], res[:])
+            if cut > 0:
+                nc.tensor.matmul(open_sums[b][:], ident[:], prod[:, 0:cut], start=False, stop=True)
+                nc.scalar.copy(res[:, 0:cut], open_sums[b][:])
+            if cut < N:
+                nc.vector.tensor_tensor(res[:, cut:N], prod[:, cut:N], translations[b][:], ADD)
+            store_queue = nc.scalar if cut > 0 else nc.sync
+            store_queue.dma_start(out_blocks[b], res[:])

@@ -8,7 +8,7 @@ KSTEPS = H // P
 HID_PIECE = 2
 TR_AHEAD = 3
 SC_AHEAD = TR_AHEAD + 1
-TENSOR_COLUMNS = [0] * (BLOCKS - 4) + [N, N, N // 2, 0]
+TENSOR_COLUMNS = [0] * (BLOCKS - 5) + [N // 2, N, N, N // 2, 0]
 
 BF16, F32, U16 = mybir.dt.bfloat16, mybir.dt.float32, mybir.dt.uint16
 MULT, ADD = mybir.AluOpType.mult, mybir.AluOpType.add

import concourse.mybir as mybir
from concourse.masks import make_identity

P = 128
C, S, N, H = 1024, 512, 384, 256
BLOCKS = C // P
KSTEPS = H // P
HID_PIECE = 2
TR_AHEAD = 3
SC_AHEAD = TR_AHEAD + 1
TENSOR_COLUMNS = [0] * (BLOCKS - 5) + [N // 2, N, N, N // 2, 0]

BF16, F32, U16 = mybir.dt.bfloat16, mybir.dt.float32, mybir.dt.uint16
MULT, ADD = mybir.AluOpType.mult, mybir.AluOpType.add
EXP = mybir.ActivationFunctionType.Exp

FLOPS = 2 * 2 * C * H * N
BYTES = 4 * C * N + 2 * H * C + 2 * 2 * H * N + 2 * P * (N // 16) + 4 * C * N


def tile_affine_coupling_layer_kernel(tc, x, hid, w_s, w_t, offs, out):
    nc = tc.nc
    with (
        tc.tile_pool(name="held", bufs=1) as held,
        tc.tile_pool(name="work", bufs=SC_AHEAD + 1) as work,
        tc.psum_pool(name="psum_sc", bufs=3) as psum_sc,
        tc.psum_pool(name="psum_tr", bufs=5) as psum_tr,
    ):
        offsets = held.tile([P, N // 16], U16, name="offsets")

        hid_pieces = hid.rearrange("(p k) (g c) -> g p k c", p=P, c=HID_PIECE * P)
        x_blocks = x.rearrange("(b p) s -> b p s", p=P)
        out_blocks = out.rearrange("(b p) n -> b p n", p=P)

        ws_sb = held.tile([P, KSTEPS, N], BF16, name="ws_sb")
        wt_sb = held.tile([P, KSTEPS, N], BF16, name="wt_sb")
        hid_sb = [
            held.tile([P, KSTEPS, HID_PIECE * P], BF16, name=f"hid{g}")
            for g in range(BLOCKS // HID_PIECE)
        ]
        x_sb = [held.tile([P, S], F32, name=f"x{b}") for b in range(BLOCKS)]

        ws_steps = w_s.rearrange("(p k) n -> k p n", p=P)
        hid_first_steps = hid.rearrange("(p k) c -> k p c", p=P)[:, :, 0 : HID_PIECE * P]
        for k in range(KSTEPS):
            nc.sync.dma_start(hid_sb[0][:, k, :], hid_first_steps[k])
            nc.sync.dma_start(ws_sb[:, k, :], ws_steps[k])
        for b in range(BLOCKS):
            nc.sync.dma_start(x_sb[b][:], x_blocks[b])
            if b == 0:
                nc.sync.dma_start(offsets[:], offs)
                nc.sync.dma_start(wt_sb[:], w_t.rearrange("(p k) n -> p k n", p=P))
            elif b == 1:
                nc.sync.dma_start(hid_sb[1][:], hid_pieces[1])
            elif b % HID_PIECE == 0 and b + HID_PIECE < BLOCKS:
                nc.sync.dma_start(hid_sb[b // HID_PIECE + 1][:], hid_pieces[b // HID_PIECE + 1])

        ident = held.tile([P, P], F32, name="ident")
        make_identity(nc, ident[:])

        scales = {}
        open_sums = {}
        translations = {}

        def hid_of(b, k):
            first = (b % HID_PIECE) * P
            return hid_sb[b // HID_PIECE][:, k, first : first + P]

        def logits(b):
            sc = psum_sc.tile([P, N], F32, name="sc")
            steps = range(KSTEPS) if b == 0 else range(KSTEPS - 1, -1, -1)
            for i, k in enumerate(steps):
                nc.tensor.matmul(
                    sc[:], hid_of(b, k), ws_sb[:, k, :], start=(i == 0), stop=(i == KSTEPS - 1)
                )
            scale = work.tile([P, N], F32, name="scale")
            nc.scalar.activation(scale[:], sc[:], EXP)
            scales[b] = scale

        def translation(b):
            cut = TENSOR_COLUMNS[b]
            for first, end, tensor_adds in ((0, cut, True), (cut, N, False)):
                if first == end:
                    continue
                tr = psum_tr.tile([P, end - first], F32, name="tr")
                for k in range(KSTEPS):
                    nc.tensor.matmul(
                        tr[:],
                        hid_of(b, k),
                        wt_sb[:, k, first:end],
                        start=(k == 0),
                        stop=(k == KSTEPS - 1 and not tensor_adds),
                    )
                if tensor_adds:
                    open_sums[b] = tr
                else:
                    tr_sb = work.tile([P, end - first], F32, name="tr_sb")
                    nc.scalar.copy(tr_sb[:], tr[:])
                    translations[b] = tr_sb

        def read_outs(b):
            if b + 1 < BLOCKS:
                logits(b + 1)
            translation(b)

        logits(0)
        for b in range(TR_AHEAD):
            read_outs(b)

        for b in range(BLOCKS):
            if b + TR_AHEAD < BLOCKS:
                read_outs(b + TR_AHEAD)
            cut = TENSOR_COLUMNS[b]

            prod = work.tile([P, N], F32, name="prod")
            nc.vector.tensor_tensor(prod[:], x_sb[b][:].indirect(offsets[:]), scales[b][:], MULT)

            res = work.tile([P, N], F32, name="res")
            if cut > 0:
                nc.tensor.matmul(open_sums[b][:], ident[:], prod[:, 0:cut], start=False, stop=True)
                nc.scalar.copy(res[:, 0:cut], open_sums[b][:])
            if cut < N:
                nc.vector.tensor_tensor(res[:, cut:N], prod[:, cut:N], translations[b][:], ADD)
            store_queue = nc.scalar if cut > 0 else nc.sync
            store_queue.dma_start(out_blocks[b], res[:])
